import numpy as np
import ml_dtypes


def mxq(x, axis, fmt="e4m3"):
    dtype, down = {"e4m3": (ml_dtypes.float8_e4m3fn, 7), "e5m2": (ml_dtypes.float8_e5m2, 14)}[fmt]
    v = np.moveaxis(np.asarray(x, np.float32).astype(ml_dtypes.bfloat16).astype(np.float64), axis, -1)
    blocks = v.reshape(v.shape[:-1] + (-1, 32))
    amax = np.abs(blocks).max(-1, keepdims=True)
    byte = np.maximum(np.where(amax > 0, np.frexp(amax)[1] - 1 + 127, 0) - down, 1)
    scale = np.exp2(byte - 127.0)
    codes = (blocks / scale).astype(np.float32).astype(dtype).astype(np.float64)
    return np.moveaxis((codes * scale).reshape(v.shape), -1, axis)


WIDE = False


def mx_kscale(k):
    if not WIDE:
        return np.ones(k)
    levels = np.array([10, -10, 5, -5, 0])
    if k % 512:
        return np.exp2(np.random.permutation(np.resize(levels, k // 32))).repeat(32)
    a = np.empty((k // 512, 16))
    for p in range(k // 512):
        a[p, :8] = np.random.permutation(np.resize(levels, 8))
        for g in range(8):
            far = levels[np.abs(levels - a[p, g]) >= 10]
            a[p, g + 8] = far[np.random.randint(len(far))]
    return np.exp2(a.ravel()).repeat(32)


BF16 = ml_dtypes.bfloat16


def bf(x):
    return np.asarray(x, np.float32).astype(BF16)


def f64(x):
    return np.asarray(x).astype(np.float64)


B, S, IQ, OQ, Q = 4, 256, 512, 512, 4


def draw0():
    s = mx_kscale(IQ)
    sw = 0.5 / np.sqrt(IQ)
    return {"x": bf((np.random.standard_normal((B, S, IQ, Q)) * s[:, None]).reshape(B, S, IQ * Q)),
            "wr": bf(np.random.standard_normal((OQ, IQ)) * sw / s),
            "wi": bf(np.random.standard_normal((OQ, IQ)) * sw / s),
            "wj": bf(np.random.standard_normal((OQ, IQ)) * sw / s),
            "wk": bf(np.random.standard_normal((OQ, IQ)) * sw / s),
            "bias": bf(np.random.standard_normal(OQ * Q) * 0.3)}


def core(x, wr, wi, wj, wk, bias):
    xq = f64(x).reshape(B * S, IQ, Q)
    xr = mxq(xq[:, :, 0], 1, "e4m3")
    xi = mxq(xq[:, :, 1], 1, "e4m3")
    xj = mxq(xq[:, :, 2], 1, "e4m3")
    xk = mxq(xq[:, :, 3], 1, "e4m3")
    qr = mxq(f64(wr), 1, "e4m3")
    qi = mxq(f64(wi), 1, "e4m3")
    qj = mxq(f64(wj), 1, "e4m3")
    qk = mxq(f64(wk), 1, "e4m3")
    Ar = xr @ qr.T
    Br = xi @ qr.T
    Cr = xj @ qr.T
    Dr = xk @ qr.T
    Ai = xr @ qi.T
    Bi = xi @ qi.T
    Aj = xr @ qj.T
    Cj = xj @ qj.T
    Ak = xr @ qk.T
    Dk = xk @ qk.T
    or_ = Ar - Bi - Cj - Dk
    oi_ = Br + Ai + Dk - Cj
    oj_ = Cr - Dk + Aj + Bi
    ok_ = Dr + Cj - Bi + Ak
    out = np.stack([or_, oi_, oj_, ok_], axis=-1).reshape(B, S, Q * OQ)
    return out + f64(bias)[None, None, :]


def e4m3fn_bytes(y):
    return np.clip(np.asarray(y, np.float64), -448.0, 448.0).astype(np.float32).astype(ml_dtypes.float8_e4m3fn).view(np.uint8)


def e4m3fn_values(b):
    return np.asarray(b, np.uint8).view(ml_dtypes.float8_e4m3fn).astype(np.float64)


def setup_inputs():
    d = draw0()
    x0 = np.asarray(d['x']).astype(np.float64)
    s = (np.max(np.abs(x0), axis=(0, 1), keepdims=True) / 448.0).astype(np.float32)
    out = {}
    for k, v in d.items():
        if k == 'x':
            out['x_bytes'] = e4m3fn_bytes(x0 / s.astype(np.float64))
            out['x_scale'] = s
        else:
            out[k] = v
    return out


def reference(x_bytes, x_scale, wr, wi, wj, wk, bias):
    return core(e4m3fn_values(x_bytes) * x_scale.astype(np.float64), wr, wi, wj, wk, bias)

@@ -1,0 +1,269 @@
+from contextlib import ExitStack
+
+import concourse.mybir as mybir
+from concourse.masks import make_identity
+
+F32 = mybir.dt.float32
+BF16 = mybir.dt.bfloat16
+U32 = mybir.dt.uint32
+U8 = mybir.dt.uint8
+FP8 = mybir.dt.float8_e4m3fn
+FP8X4 = mybir.dt.float8_e4m3fn_x4
+MULT = mybir.AluOpType.mult
+ADD = mybir.AluOpType.add
+
+P = 128
+ROWS = 1024
+IQ = 512
+OQ = 512
+Q = 4
+COLS = IQ * Q
+ROW_TILES = ROWS // P
+O_BLOCKS = OQ // P
+FLOPS = 10 * 2 * ROWS * IQ * OQ
+
+N_BLOCKS = 7
+FIRST_CAST_SPLIT = 640
+GROUPS = (
+    (0, 128, (2, 6, 0, 1)),
+    (128, 128, (5, 2, 0, 4)),
+    (256, 256, (3, 5, 2, 1)),
+)
+
+
+def tile_quaternionlinear_pa_kernel(tc, x_bytes, x_scale, wr, wi, wj, wk, bias, out):
+    nc = tc.nc
+    x_rows = x_bytes.flatten_outer_dims()
+    out_rows = out.flatten_outer_dims()
+    weights = (wr, wj, wk, wi)
+
+    with ExitStack() as ctx:
+        const = ctx.enter_context(tc.tile_pool(name="const", bufs=1))
+        xb_pool = ctx.enter_context(tc.tile_pool(name="xb_pool", bufs=3))
+        xp_pool = ctx.enter_context(tc.tile_pool(name="xp_pool", bufs=2))
+        xg_pool = ctx.enter_context(tc.tile_pool(name="xg_pool", bufs=2))
+        xc_pool = ctx.enter_context(tc.tile_pool(name="xc_pool", bufs=2))
+        res_pool = ctx.enter_context(tc.tile_pool(name="res_pool", bufs=6))
+        psum = ctx.enter_context(tc.psum_pool(name="psum", bufs=8))
+        ctx.enter_context(tc.manual_schedule())
+
+        ident = const.tile([P, P], F32, name="ident")
+        scale16 = const.tile([P, 16], F32, name="scale16")
+        bias_all = const.tile([P, COLS], BF16, name="bias_all")
+        x_codes_in = [const.tile([P, COLS], U8, name="x_codes_in_%d" % i) for i in range(ROW_TILES)]
+        w_raw = [const.tile([P, 4, IQ], BF16, name="w_raw_%d" % ob) for ob in range(O_BLOCKS)]
+        w_grouped = [
+            const.tile([P, N_BLOCKS * 512], BF16, name="w_grouped_%d" % ob, align_bytes=64)
+            for ob in range(O_BLOCKS)
+        ]
+        w_codes = [
+            const.tile([P, N_BLOCKS * P], U32, name="w_codes_%d" % ob, align_bytes=64)
+            for ob in range(O_BLOCKS)
+        ]
+        w_scales = [
+            const.tile([P, N_BLOCKS * P], U8, name="w_scales_%d" % ob, align_bytes=64)
+            for ob in range(O_BLOCKS)
+        ]
+
+        def load_x(i):
+            nc.sync.dma_start(out=x_codes_in[i][:], in_=x_rows[P * i : P * (i + 1), :])
+
+        def load_w(ob):
+            for s in range(4):
+                nc.sync.dma_start(out=w_raw[ob][:, s, :], in_=weights[s][P * ob : P * (ob + 1), :])
+
+        make_identity(nc, ident[:])
+        load_x(0)
+        nc.sync.dma_start(out=scale16[:], in_=x_scale.rearrange("a b (p e) -> (a b p) e", e=16))
+        load_x(1)
+        load_w(0)
+        load_w(1)
+        load_w(2)
+        load_w(3)
+        load_x(2)
+        nc.sync.dma_start(out=bias_all[:], in_=bias.partition_broadcast(P))
+        for i in range(3, ROW_TILES):
+            load_x(i)
+
+        scale_views = [
+            scale16[:].rearrange("p (t h e) -> p h e t", h=2, e=2)[:, h].unsqueeze(2).to_broadcast([P, 2, P, 4])
+            for h in range(2)
+        ]
+
+        xb = {}
+        xt = {}
+        xp = {}
+        xg = {}
+        xc = {}
+        xs = {}
+        wt = {}
+        acc = {}
+
+        def cast(i):
+            xb[i] = xb_pool.tile([P, COLS], BF16, name="xb", tag="xb")
+            codes = x_codes_in[i][:].bitcast(FP8)
+            split = FIRST_CAST_SPLIT if i == 0 else COLS
+            nc.scalar.copy(out=xb[i][:, 0:split], in_=codes[:, 0:split])
+            if split < COLS:
+                nc.vector.tensor_copy(out=xb[i][:, split:COLS], in_=codes[:, split:COLS])
+
+        def regroup(i):
+            xp[i] = xp_pool.tile([P, 8, P], F32, name="xp", tag="xp")
+            nc.scalar.copy(out=xp[i][:], in_=xb[i][:].bitcast(F32).rearrange("p (j q) -> p q j", q=8))
+
+        def x_transpose(i):
+            words = xb[i][:].bitcast(F32)
+            xt[i] = []
+            for h in range(2):
+                bank = psum.tile([P, 4, P], F32, name="bank", tag="bank")
+                for t in range(4):
+                    if i in xp:
+                        nc.tensor.transpose(bank[:, t, :], xp[i][:, 2 * t + h, :], ident[:])
+                    else:
+                        nc.tensor.transpose(bank[:, t, :], words[:, 2 * t + h : COLS // 2 : 8], ident[:])
+                xt[i].append(bank)
+
+        def x_scale_out(i):
+            xg[i] = xg_pool.tile([P, COLS], BF16, name="xg", tag="xg", align_bytes=64)
+            grouped = xg[i][:].rearrange("p (c n t) -> p c n t", c=4, t=4)
+            for h in range(2):
+                halves = xt[i][h][:].rearrange("p t n -> p (t n)").bitcast(BF16)
+                nc.vector.tensor_tensor(
+                    out=grouped[:, 2 * h : 2 * h + 2],
+                    in0=halves.rearrange("p (t n e) -> p e n t", t=4, e=2),
+                    in1=scale_views[h],
+                    op=MULT,
+                )
+
+        def x_quantize(i):
+            xc[i] = xc_pool.tile([P, 4 * P], U32, name="xc", tag="xc", align_bytes=64)
+            xs[i] = xc_pool.tile([P, 4 * P], U8, name="xs", tag="xs", align_bytes=64)
+            nc.vector.quantize_mx(out=xc[i][:].bitcast(FP8X4), scales=xs[i][:], in_=xg[i][:])
+
+        def w_transpose(ob):
+            wt[ob] = []
+            for b in range(2):
+                bank = psum.tile([P, 4, P], F32, name="bank", tag="bank")
+                for s2 in range(2):
+                    words = w_raw[ob][:, 2 * b + s2, :].bitcast(F32)
+                    for u in range(2):
+                        nc.tensor.transpose(bank[:, 2 * s2 + u, :], words[:, u : IQ // 2 : 2], ident[:])
+                wt[ob].append(bank)
+
+        def w_out(ob):
+            words = w_grouped[ob][:].bitcast(F32)
+            for b in range(2):
+                first = (2 + 2 * b) * 256
+                nc.scalar.copy(
+                    out=words[:, first : first + 512].rearrange("p (s o u) -> p s o u", s=2, u=2),
+                    in_=wt[ob][b][:].rearrange("p (s u) o -> p s o u", s=2),
+                )
+
+        def w_negate(ob):
+            g = w_grouped[ob]
+            nc.vector.tensor_scalar(out=g[:, 0:1024], in0=g[:, 1536:2560], scalar1=-1.0, scalar2=None, op0=MULT)
+            nc.vector.tensor_scalar(out=g[:, 3072:3584], in0=g[:, 2560:3072], scalar1=-1.0, scalar2=None, op0=MULT)
+
+        def w_quantize(ob):
+            for first, count in ((2, 4), (0, 2), (6, 1)):
+                cols = slice(first * P, (first + count) * P)
+                nc.vector.quantize_mx(
+                    out=w_codes[ob][:, cols].bitcast(FP8X4),
+                    scales=w_scales[ob][:, cols],
+                    in_=w_grouped[ob][:, first * 512 : (first + count) * 512],
+                )
+
+        def multiply(i, ob):
+            bank = psum.tile([P, 512], F32, name="bank", tag="bank")
+            acc[(i, ob)] = bank
+            for col0, width, blocks in GROUPS:
+                for cp in range(4):
+                    x_cols = slice(P * cp, P * (cp + 1))
+                    w_cols = slice(P * blocks[cp], P * blocks[cp] + width)
+                    nc.tensor.matmul_mx(
+                        out=bank[:, col0 : col0 + width],
+                        lhsT=xc[i][:, x_cols].bitcast(FP8X4),
+                        lhsT_scale=xs[i][:, x_cols],
+                        rhs=w_codes[ob][:, w_cols].bitcast(FP8X4),
+                        rhs_scale=w_scales[ob][:, w_cols],
+                        start=(cp == 0),
+                        stop=(cp == 3),
+                    )
+
+        def by_gpsimd(i, ob):
+            return ob == 3 and i < ROW_TILES - 1
+
+        def finish(i, ob):
+            res = res_pool.tile([P, 512], F32, name="res", tag="res")
+            cols = slice(512 * ob, 512 * (ob + 1))
+            sums = acc[(i, ob)][:].rearrange("p (c o) -> p o c", c=4)
+            if by_gpsimd(i, ob):
+                nc.scalar.copy(out=res[:].rearrange("p (o c) -> p o c", c=4), in_=sums)
+                nc.gpsimd.tensor_tensor(out=res[:], in0=res[:], in1=bias_all[:, cols], op=ADD)
+            else:
+                nc.vector.tensor_tensor(
+                    out=res[:].rearrange("p (o c) -> p o c", c=4),
+                    in0=sums,
+                    in1=bias_all[:, cols].rearrange("p (o c) -> p o c", c=4),
+                    op=ADD,
+                )
+            nc.sync.dma_start(out=out_rows[P * i : P * (i + 1), cols], in_=res[:])
+
+        cast(0)
+        x_transpose(0)
+        cast(1)
+        w_transpose(0)
+        w_out(0)
+        x_scale_out(0)
+        x_quantize(0)
+        w_negate(0)
+        w_quantize(0)
+        for ob in range(1, O_BLOCKS):
+            w_transpose(ob)
+            w_out(ob)
+            w_negate(ob)
+            w_quantize(ob)
+        x_transpose(1)
+        cast(2)
+        x_scale_out(1)
+        x_quantize(1)
+
+        waiting = []
+        for i in range(ROW_TILES):
+            more = i >= 1 and i + 1 < ROW_TILES
+            if more:
+                x_transpose(i + 1)
+            if i >= 1 and by_gpsimd(i - 1, 3):
+                finish(i - 1, 3)
+            if i + 2 < ROW_TILES and i >= 1:
+                cast(i + 2)
+                regroup(i + 2)
+            if more:
+                x_scale_out(i + 1)
+            for ob in range(O_BLOCKS):
+                if not by_gpsimd(i, ob):
+                    waiting.append((i, ob))
+            share = []
+            if i >= 1:
+                share = [b for b in waiting if b <= (i, 2)][:4]
+            for b in share:
+                waiting.remove(b)
+            early = [b for b in share if b[0] < i]
+            late = [b for b in share if b[0] == i]
+            quantized = not more
+            for b in early:
+                finish(b[0], b[1])
+                if not quantized:
+                    x_quantize(i + 1)
+                    quantized = True
+            for ob in range(O_BLOCKS):
+                multiply(i, ob)
+            for b in late:
+                finish(b[0], b[1])
+                if not quantized:
+                    x_quantize(i + 1)
+                    quantized = True
+            if not quantized:
+                x_quantize(i + 1)
+        for b in waiting:
+            finish(b[0], b[1])

@@ -42,8 +42,9 @@ def tile_quaternionlinear_pa_kernel(tc, x_bytes, x_scale, wr, wi, wj, wk, bias, 
         xb_pool = ctx.enter_context(tc.tile_pool(name="xb_pool", bufs=3))
         xp_pool = ctx.enter_context(tc.tile_pool(name="xp_pool", bufs=2))
         xg_pool = ctx.enter_context(tc.tile_pool(name="xg_pool", bufs=2))
-        xc_pool = ctx.enter_context(tc.tile_pool(name="xc_pool", bufs=2))
-        res_pool = ctx.enter_context(tc.tile_pool(name="res_pool", bufs=6))
+        xc_pool = ctx.enter_context(tc.tile_pool(name="xc_pool", bufs=3))
+        res_pool = ctx.enter_context(tc.tile_pool(name="res_pool", bufs=10))
+        held_pool = ctx.enter_context(tc.tile_pool(name="held_pool", bufs=4))
         psum = ctx.enter_context(tc.psum_pool(name="psum", bufs=8))
         ctx.enter_context(tc.manual_schedule())
 
@@ -78,11 +79,12 @@ def tile_quaternionlinear_pa_kernel(tc, x_bytes, x_scale, wr, wi, wj, wk, bias, 
         load_x(1)
         load_w(0)
         load_w(1)
+        load_x(2)
         load_w(2)
         load_w(3)
-        load_x(2)
+        load_x(3)
         nc.sync.dma_start(out=bias_all[:], in_=bias.partition_broadcast(P))
-        for i in range(3, ROW_TILES):
+        for i in range(4, ROW_TILES):
             load_x(i)
 
         scale_views = [
@@ -190,24 +192,33 @@ def tile_quaternionlinear_pa_kernel(tc, x_bytes, x_scale, wr, wi, wj, wk, bias, 
                         stop=(cp == 3),
                     )
 
-        def by_gpsimd(i, ob):
-            return ob == 3 and i < ROW_TILES - 1
+        res = {}
+
+        def store(i, ob):
+            nc.sync.dma_start(out=out_rows[P * i : P * (i + 1), 512 * ob : 512 * (ob + 1)], in_=res[(i, ob)][:])
 
         def finish(i, ob):
-            res = res_pool.tile([P, 512], F32, name="res", tag="res")
-            cols = slice(512 * ob, 512 * (ob + 1))
-            sums = acc[(i, ob)][:].rearrange("p (c o) -> p o c", c=4)
-            if by_gpsimd(i, ob):
-                nc.scalar.copy(out=res[:].rearrange("p (o c) -> p o c", c=4), in_=sums)
-                nc.gpsimd.tensor_tensor(out=res[:], in0=res[:], in1=bias_all[:, cols], op=ADD)
-            else:
-                nc.vector.tensor_tensor(
-                    out=res[:].rearrange("p (o c) -> p o c", c=4),
-                    in0=sums,
-                    in1=bias_all[:, cols].rearrange("p (o c) -> p o c", c=4),
-                    op=ADD,
-                )
-            nc.sync.dma_start(out=out_rows[P * i : P * (i + 1), cols], in_=res[:])
+            res[(i, ob)] = res_pool.tile([P, 512], F32, name="res", tag="res")
+            nc.vector.tensor_tensor(
+                out=res[(i, ob)][:].rearrange("p (o c) -> p o c", c=4),
+                in0=acc[(i, ob)][:].rearrange("p (c o) -> p o c", c=4),
+                in1=bias_all[:, 512 * ob : 512 * (ob + 1)].rearrange("p (o c) -> p o c", c=4),
+                op=ADD,
+            )
+            store(i, ob)
+
+        def copy_out(i, ob, pool):
+            res[(i, ob)] = pool.tile([P, 512], F32, name="res", tag="res")
+            nc.scalar.copy(
+                out=res[(i, ob)][:].rearrange("p (o c) -> p o c", c=4),
+                in_=acc[(i, ob)][:].rearrange("p (c o) -> p o c", c=4),
+            )
+
+        def add_bias(engine, i, ob):
+            engine.tensor_tensor(
+                out=res[(i, ob)][:], in0=res[(i, ob)][:], in1=bias_all[:, 512 * ob : 512 * (ob + 1)], op=ADD
+            )
+            store(i, ob)
 
         cast(0)
         x_transpose(0)
@@ -218,52 +229,78 @@ def tile_quaternionlinear_pa_kernel(tc, x_bytes, x_scale, wr, wi, wj, wk, bias, 
         x_quantize(0)
         w_negate(0)
         w_quantize(0)
-        for ob in range(1, O_BLOCKS):
-            w_transpose(ob)
-            w_out(ob)
-            w_negate(ob)
-            w_quantize(ob)
+        w_transpose(1)
+        w_out(1)
+        w_negate(1)
+        w_quantize(1)
         x_transpose(1)
         cast(2)
+        w_transpose(2)
+        w_out(2)
+        w_transpose(3)
+        w_out(3)
         x_scale_out(1)
         x_quantize(1)
+        multiply(0, 0)
+        multiply(0, 1)
+        x_transpose(2)
+        w_negate(2)
+        w_quantize(2)
+        w_negate(3)
+        w_quantize(3)
+        copy_out(0, 0, held_pool)
+        copy_out(0, 1, held_pool)
+        cast(3)
+        regroup(3)
+        multiply(1, 0)
+        multiply(1, 1)
+        copy_out(1, 0, held_pool)
+        copy_out(1, 1, held_pool)
+        x_scale_out(2)
+        x_quantize(2)
+        multiply(0, 2)
+        multiply(1, 2)
+        multiply(0, 3)
+        multiply(1, 3)
+        finish(0, 2)
+        finish(1, 2)
+        copy_out(0, 3, res_pool)
+        add_bias(nc.gpsimd, 0, 3)
+        held = [(0, 0), (0, 1), (1, 0), (1, 1)]
 
-        waiting = []
-        for i in range(ROW_TILES):
-            more = i >= 1 and i + 1 < ROW_TILES
+        for i in range(2, ROW_TILES):
+            more = i + 1 < ROW_TILES
             if more:
                 x_transpose(i + 1)
-            if i >= 1 and by_gpsimd(i - 1, 3):
-                finish(i - 1, 3)
-            if i + 2 < ROW_TILES and i >= 1:
+            copy_out(i - 1, 3, res_pool)
+            add_bias(nc.gpsimd, i - 1, 3)
+            if i + 2 < ROW_TILES:
                 cast(i + 2)
                 regroup(i + 2)
             if more:
                 x_scale_out(i + 1)
-            for ob in range(O_BLOCKS):
-                if not by_gpsimd(i, ob):
-                    waiting.append((i, ob))
-            share = []
-            if i >= 1:
-                share = [b for b in waiting if b <= (i, 2)][:4]
-            for b in share:
-                waiting.remove(b)
-            early = [b for b in share if b[0] < i]
-            late = [b for b in share if b[0] == i]
-            quantized = not more
-            for b in early:
-                finish(b[0], b[1])
-                if not quantized:
-                    x_quantize(i + 1)
-                    quantized = True
+            if i > 2:
+                finish(i - 1, 2)
+            if more:
+                x_quantize(i + 1)
+            if held:
+                b = held.pop(0)
+                add_bias(nc.vector, b[0], b[1])
             for ob in range(O_BLOCKS):
                 multiply(i, ob)
-            for b in late:
-                finish(b[0], b[1])
-                if not quantized:
-                    x_quantize(i + 1)
-                    quantized = True
-            if not quantized:
-                x_quantize(i + 1)
-        for b in waiting:
-            finish(b[0], b[1])
+            finish(i, 0)
+            finish(i, 1)
+        finish(ROW_TILES - 1, 2)
+        last = (ROW_TILES - 1, O_BLOCKS - 1)
+        res[last] = res_pool.tile([P, 512], F32, name="res", tag="res")
+        for half in range(2):
+            o_part = slice(64 * half, 64 * (half + 1))
+            cols = slice(256 * half, 256 * (half + 1))
+            first = 512 * last[1] + 256 * half
+            nc.vector.tensor_tensor(
+                out=res[last][:, cols].rearrange("p (o c) -> p o c", c=4),
+                in0=acc[last][:].rearrange("p (c o) -> p o c", c=4)[:, o_part, :],
+                in1=bias_all[:, first : first + 256].rearrange("p (o c) -> p o c", c=4),
+                op=ADD,
+            )
+            nc.sync.dma_start(out=out_rows[P * last[0] : P * (last[0] + 1), first : first + 256], in_=res[last][:, cols])

@@ -79,9 +79,9 @@ def tile_quaternionlinear_pa_kernel(tc, x_bytes, x_scale, wr, wi, wj, wk, bias, 
         load_x(1)
         load_w(0)
         load_w(1)
-        load_x(2)
         load_w(2)
         load_w(3)
+        load_x(2)
         load_x(3)
         nc.sync.dma_start(out=bias_all[:], in_=bias.partition_broadcast(P))
         for i in range(4, ROW_TILES):
@@ -140,7 +140,14 @@ def tile_quaternionlinear_pa_kernel(tc, x_bytes, x_scale, wr, wi, wj, wk, bias, 
         def x_quantize(i):
             xc[i] = xc_pool.tile([P, 4 * P], U32, name="xc", tag="xc", align_bytes=64)
             xs[i] = xc_pool.tile([P, 4 * P], U8, name="xs", tag="xs", align_bytes=64)
-            nc.vector.quantize_mx(out=xc[i][:].bitcast(FP8X4), scales=xs[i][:], in_=xg[i][:])
+            parts = 2 if i < 3 else 1
+            for part in range(parts):
+                cols = slice(4 * P // parts * part, 4 * P // parts * (part + 1))
+                nc.vector.quantize_mx(
+                    out=xc[i][:, cols].bitcast(FP8X4),
+                    scales=xs[i][:, cols],
+                    in_=xg[i][:, 4 * cols.start : 4 * cols.stop],
+                )
 
         def w_transpose(ob):
             wt[ob] = []
@@ -234,9 +241,9 @@ def tile_quaternionlinear_pa_kernel(tc, x_bytes, x_scale, wr, wi, wj, wk, bias, 
         w_negate(1)
         w_quantize(1)
         x_transpose(1)
-        cast(2)
         w_transpose(2)
         w_out(2)
+        cast(2)
         w_transpose(3)
         w_out(3)
         x_scale_out(1)

@@ -23,7 +23,7 @@ O_BLOCKS = OQ // P
 FLOPS = 10 * 2 * ROWS * IQ * OQ
 
 N_BLOCKS = 7
-FIRST_CAST_SPLIT = 640
+FIRST_CAST_SPLIT = 768
 GROUPS = (
     (0, 128, (2, 6, 0, 1)),
     (128, 128, (5, 2, 0, 4)),
@@ -182,9 +182,13 @@ def tile_quaternionlinear_pa_kernel(tc, x_bytes, x_scale, wr, wi, wj, wk, bias, 
                     in_=w_grouped[ob][:, first * 512 : (first + count) * 512],
                 )
 
+        def reserve(i, ob):
+            acc[(i, ob)] = psum.tile([P, 512], F32, name="bank", tag="bank")
+
         def multiply(i, ob):
-            bank = psum.tile([P, 512], F32, name="bank", tag="bank")
-            acc[(i, ob)] = bank
+            if (i, ob) not in acc:
+                reserve(i, ob)
+            bank = acc[(i, ob)]
             for col0, width, blocks in GROUPS:
                 for cp in range(4):
                     x_cols = slice(P * cp, P * (cp + 1))
@@ -250,6 +254,8 @@ def tile_quaternionlinear_pa_kernel(tc, x_bytes, x_scale, wr, wi, wj, wk, bias, 
         x_quantize(1)
         multiply(0, 0)
         multiply(0, 1)
+        reserve(1, 0)
+        reserve(1, 1)
         x_transpose(2)
         w_negate(2)
         w_quantize(2)

@@ -23,11 +23,20 @@ O_BLOCKS = OQ // P
 FLOPS = 10 * 2 * ROWS * IQ * OQ
 
 N_BLOCKS = 7
+CODE_BLOCKS = 12
+FIRST_CODE = 3
+SECOND = ((0, 1), (1, 4), (2, 0), (10, 2), (11, 5))
+WIDE_BLOCKS = (0, 1)
+FIRST_WIDE = 2
 FIRST_CAST_SPLIT = 768
 GROUPS = (
-    (0, 128, (2, 6, 0, 1)),
-    (128, 128, (5, 2, 0, 4)),
-    (256, 256, (3, 5, 2, 1)),
+    (0, 128, (5, 9, 3, 4)),
+    (128, 128, (8, 5, 3, 7)),
+    (256, 256, (6, 8, 5, 4)),
+)
+GROUPS_WIDE = (
+    (0, 256, (10, 9, 2, 0)),
+    (256, 256, (6, 8, 5, 4)),
 )
 
 
@@ -58,11 +67,11 @@ def tile_quaternionlinear_pa_kernel(tc, x_bytes, x_scale, wr, wi, wj, wk, bias, 
             for ob in range(O_BLOCKS)
         ]
         w_codes = [
-            const.tile([P, N_BLOCKS * P], U32, name="w_codes_%d" % ob, align_bytes=64)
+            const.tile([P, CODE_BLOCKS * P], U32, name="w_codes_%d" % ob, align_bytes=64)
             for ob in range(O_BLOCKS)
         ]
         w_scales = [
-            const.tile([P, N_BLOCKS * P], U8, name="w_scales_%d" % ob, align_bytes=64)
+            const.tile([P, CODE_BLOCKS * P], U8, name="w_scales_%d" % ob, align_bytes=64)
             for ob in range(O_BLOCKS)
         ]
 
@@ -175,11 +184,20 @@ def tile_quaternionlinear_pa_kernel(tc, x_bytes, x_scale, wr, wi, wj, wk, bias, 
 
         def w_quantize(ob):
             for first, count in ((2, 4), (0, 2), (6, 1)):
-                cols = slice(first * P, (first + count) * P)
+                cols = slice((FIRST_CODE + first) * P, (FIRST_CODE + first + count) * P)
                 nc.vector.quantize_mx(
                     out=w_codes[ob][:, cols].bitcast(FP8X4),
                     scales=w_scales[ob][:, cols],
                     in_=w_grouped[ob][:, first * 512 : (first + count) * 512],
+                )
+
+        def w_quantize_again(ob):
+            for place, block in SECOND:
+                cols = slice(place * P, (place + 1) * P)
+                nc.vector.quantize_mx(
+                    out=w_codes[ob][:, cols].bitcast(FP8X4),
+                    scales=w_scales[ob][:, cols],
+                    in_=w_grouped[ob][:, block * 512 : (block + 1) * 512],
                 )
 
         def reserve(i, ob):
@@ -189,7 +207,7 @@ def tile_quaternionlinear_pa_kernel(tc, x_bytes, x_scale, wr, wi, wj, wk, bias, 
             if (i, ob) not in acc:
                 reserve(i, ob)
             bank = acc[(i, ob)]
-            for col0, width, blocks in GROUPS:
+            for col0, width, blocks in GROUPS_WIDE if i >= FIRST_WIDE and ob in WIDE_BLOCKS else GROUPS:
                 for cp in range(4):
                     x_cols = slice(P * cp, P * (cp + 1))
                     w_cols = slice(P * blocks[cp], P * blocks[cp] + width)
@@ -271,6 +289,8 @@ def tile_quaternionlinear_pa_kernel(tc, x_bytes, x_scale, wr, wi, wj, wk, bias, 
         copy_out(1, 1, held_pool)
         x_scale_out(2)
         x_quantize(2)
+        w_quantize_again(0)
+        w_quantize_again(1)
         multiply(0, 2)
         multiply(1, 2)
         multiply(0, 3)

@@ -29,6 +29,7 @@ SECOND = ((0, 1), (1, 4), (2, 0), (10, 2), (11, 5))
 WIDE_BLOCKS = (0, 1)
 FIRST_WIDE = 2
 FIRST_CAST_SPLIT = 768
+WARM_PASSES = 5
 GROUPS = (
     (0, 128, (5, 9, 3, 4)),
     (128, 128, (8, 5, 3, 7)),
@@ -59,6 +60,7 @@ def tile_quaternionlinear_pa_kernel(tc, x_bytes, x_scale, wr, wi, wj, wk, bias, 
 
         ident = const.tile([P, P], F32, name="ident")
         scale16 = const.tile([P, 16], F32, name="scale16")
+        zeros = const.tile([P, 512], BF16, name="zeros")
         bias_all = const.tile([P, COLS], BF16, name="bias_all")
         x_codes_in = [const.tile([P, COLS], U8, name="x_codes_in_%d" % i) for i in range(ROW_TILES)]
         w_raw = [const.tile([P, 4, IQ], BF16, name="w_raw_%d" % ob) for ob in range(O_BLOCKS)]
@@ -83,6 +85,7 @@ def tile_quaternionlinear_pa_kernel(tc, x_bytes, x_scale, wr, wi, wj, wk, bias, 
                 nc.sync.dma_start(out=w_raw[ob][:, s, :], in_=weights[s][P * ob : P * (ob + 1), :])
 
         make_identity(nc, ident[:])
+        nc.vector.memset(zeros[:], 0.0)
         load_x(0)
         nc.sync.dma_start(out=scale16[:], in_=x_scale.rearrange("a b (p e) -> (a b p) e", e=16))
         load_x(1)
@@ -249,6 +252,9 @@ def tile_quaternionlinear_pa_kernel(tc, x_bytes, x_scale, wr, wi, wj, wk, bias, 
             )
             store(i, ob)
 
+        warm = psum.tile([P, 512], F32, name="bank", tag="bank")
+        for w_pass in range(WARM_PASSES):
+            nc.tensor.matmul(out=warm[:], lhsT=zeros[:, 0:P], rhs=zeros[:], start=True, stop=True)
         cast(0)
         x_transpose(0)
         cast(1)

@@ -29,7 +29,7 @@ SECOND = ((0, 1), (1, 4), (2, 0), (10, 2), (11, 5))
 WIDE_BLOCKS = (0, 1)
 FIRST_WIDE = 2
 FIRST_CAST_SPLIT = 768
-WARM_PASSES = 5
+WARM_PASSES = 6
 GROUPS = (
     (0, 128, (5, 9, 3, 4)),
     (128, 128, (8, 5, 3, 7)),
@@ -84,8 +84,8 @@ def tile_quaternionlinear_pa_kernel(tc, x_bytes, x_scale, wr, wi, wj, wk, bias, 
             for s in range(4):
                 nc.sync.dma_start(out=w_raw[ob][:, s, :], in_=weights[s][P * ob : P * (ob + 1), :])
 
+        nc.gpsimd.memset(zeros[:], 0.0)
         make_identity(nc, ident[:])
-        nc.vector.memset(zeros[:], 0.0)
         load_x(0)
         nc.sync.dma_start(out=scale16[:], in_=x_scale.rearrange("a b (p e) -> (a b p) e", e=16))
         load_x(1)

@@ -69,11 +69,11 @@ def tile_quaternionlinear_pa_kernel(tc, x_bytes, x_scale, wr, wi, wj, wk, bias, 
             for ob in range(O_BLOCKS)
         ]
         w_codes = [
-            const.tile([P, CODE_BLOCKS * P], U32, name="w_codes_%d" % ob, align_bytes=64)
+            const.tile([P, CODE_BLOCKS * P], U32, name="w_codes_%d" % ob, align_bytes=256)
             for ob in range(O_BLOCKS)
         ]
         w_scales = [
-            const.tile([P, CODE_BLOCKS * P], U8, name="w_scales_%d" % ob, align_bytes=64)
+            const.tile([P, CODE_BLOCKS * P], U8, name="w_scales_%d" % ob, align_bytes=256)
             for ob in range(O_BLOCKS)
         ]
 
@@ -150,8 +150,8 @@ def tile_quaternionlinear_pa_kernel(tc, x_bytes, x_scale, wr, wi, wj, wk, bias, 
                 )
 
         def x_quantize(i):
-            xc[i] = xc_pool.tile([P, 4 * P], U32, name="xc", tag="xc", align_bytes=64)
-            xs[i] = xc_pool.tile([P, 4 * P], U8, name="xs", tag="xs", align_bytes=64)
+            xc[i] = xc_pool.tile([P, 4 * P], U32, name="xc", tag="xc", align_bytes=256)
+            xs[i] = xc_pool.tile([P, 4 * P], U8, name="xs", tag="xs", align_bytes=256)
             parts = 2 if i < 3 else 1
             for part in range(parts):
                 cols = slice(4 * P // parts * part, 4 * P // parts * (part + 1))

@@ -210,19 +210,20 @@ def tile_quaternionlinear_pa_kernel(tc, x_bytes, x_scale, wr, wi, wj, wk, bias, 
             if (i, ob) not in acc:
                 reserve(i, ob)
             bank = acc[(i, ob)]
-            for col0, width, blocks in GROUPS_WIDE if i >= FIRST_WIDE and ob in WIDE_BLOCKS else GROUPS:
-                for cp in range(4):
-                    x_cols = slice(P * cp, P * (cp + 1))
-                    w_cols = slice(P * blocks[cp], P * blocks[cp] + width)
-                    nc.tensor.matmul_mx(
-                        out=bank[:, col0 : col0 + width],
-                        lhsT=xc[i][:, x_cols].bitcast(FP8X4),
-                        lhsT_scale=xs[i][:, x_cols],
-                        rhs=w_codes[ob][:, w_cols].bitcast(FP8X4),
-                        rhs_scale=w_scales[ob][:, w_cols],
-                        start=(cp == 0),
-                        stop=(cp == 3),
-                    )
+            groups = GROUPS_WIDE if i >= FIRST_WIDE and ob in WIDE_BLOCKS else GROUPS
+            passes = [(cp, col0, width, blocks[cp]) for cp in range(4) for col0, width, blocks in groups]
+            for number, (cp, col0, width, block) in enumerate(passes):
+                x_cols = slice(P * cp, P * (cp + 1))
+                w_cols = slice(P * block, P * block + width)
+                nc.tensor.matmul_mx(
+                    out=bank[:, col0 : col0 + width],
+                    lhsT=xc[i][:, x_cols].bitcast(FP8X4),
+                    lhsT_scale=xs[i][:, x_cols],
+                    rhs=w_codes[ob][:, w_cols].bitcast(FP8X4),
+                    rhs_scale=w_scales[ob][:, w_cols],
+                    start=(number == 0),
+                    stop=(number == len(passes) - 1),
+                )
 
         res = {}
 

@@ -22,22 +22,24 @@ ROW_TILES = ROWS // P
 O_BLOCKS = OQ // P
 FLOPS = 10 * 2 * ROWS * IQ * OQ
 
-N_BLOCKS = 7
-CODE_BLOCKS = 12
-FIRST_CODE = 3
-SECOND = ((0, 1), (1, 4), (2, 0), (10, 2), (11, 5))
-WIDE_BLOCKS = (0, 1)
+N_BLOCKS = 8
+CODE_BLOCKS = 9
+FIRST_CODE = 1
+SECOND = ((0, 2), (8, 6))
 FIRST_WIDE = 2
 FIRST_CAST_SPLIT = 768
 WARM_PASSES = 6
-GROUPS = (
-    (0, 128, (5, 9, 3, 4)),
-    (128, 128, (8, 5, 3, 7)),
-    (256, 256, (6, 8, 5, 4)),
+RUNS = (
+    ((0, 128, 3), (128, 128, 1), (256, 256, 4)),
+    ((0, 256, 2), (256, 256, 1)),
+    ((0, 128, 7), (128, 128, 7), (256, 256, 3)),
+    ((0, 128, 6), (128, 256, 5), (384, 128, 3)),
 )
-GROUPS_WIDE = (
-    (0, 256, (10, 9, 2, 0)),
-    (256, 256, (6, 8, 5, 4)),
+RUNS_WIDE = (
+    ((0, 256, 0), (256, 256, 4)),
+    ((0, 256, 2), (256, 256, 1)),
+    ((0, 256, 7), (256, 256, 3)),
+    ((0, 128, 6), (128, 256, 5), (384, 128, 3)),
 )
 
 
@@ -45,7 +47,7 @@ def tile_quaternionlinear_pa_kernel(tc, x_bytes, x_scale, wr, wi, wj, wk, bias, 
     nc = tc.nc
     x_rows = x_bytes.flatten_outer_dims()
     out_rows = out.flatten_outer_dims()
-    weights = (wr, wj, wk, wi)
+    weights = (wr, wj, wi, wk)
 
     with ExitStack() as ctx:
         const = ctx.enter_context(tc.tile_pool(name="const", bufs=1))
@@ -173,17 +175,18 @@ def tile_quaternionlinear_pa_kernel(tc, x_bytes, x_scale, wr, wi, wj, wk, bias, 
 
         def w_out(ob):
             words = w_grouped[ob][:].bitcast(F32)
+            outs = (
+                words[:, 512:1024].rearrange("p (s o u) -> p s o u", s=2, u=2),
+                words.rearrange("p (s x) -> p s x", s=2)[:, :, 0:256].rearrange("p s (o u) -> p s o u", u=2),
+            )
             for b in range(2):
-                first = (2 + 2 * b) * 256
-                nc.scalar.copy(
-                    out=words[:, first : first + 512].rearrange("p (s o u) -> p s o u", s=2, u=2),
-                    in_=wt[ob][b][:].rearrange("p (s u) o -> p s o u", s=2),
-                )
+                nc.scalar.copy(out=outs[b], in_=wt[ob][b][:].rearrange("p (s u) o -> p s o u", s=2))
 
         def w_negate(ob):
             g = w_grouped[ob]
-            nc.vector.tensor_scalar(out=g[:, 0:1024], in0=g[:, 1536:2560], scalar1=-1.0, scalar2=None, op0=MULT)
-            nc.vector.tensor_scalar(out=g[:, 3072:3584], in0=g[:, 2560:3072], scalar1=-1.0, scalar2=None, op0=MULT)
+            halves = g[:].rearrange("p (s x) -> p s x", s=2)
+            nc.vector.tensor_scalar(out=halves[:, :, 512:1024], in0=halves[:, :, 0:512], scalar1=-1.0, scalar2=None, op0=MULT)
+            nc.vector.tensor_scalar(out=g[:, 3072:3584], in0=g[:, 1536:2048], scalar1=-1.0, scalar2=None, op0=MULT)
 
         def w_quantize(ob):
             for first, count in ((2, 4), (0, 2), (6, 1)):
@@ -210,8 +213,8 @@ def tile_quaternionlinear_pa_kernel(tc, x_bytes, x_scale, wr, wi, wj, wk, bias, 
             if (i, ob) not in acc:
                 reserve(i, ob)
             bank = acc[(i, ob)]
-            groups = GROUPS_WIDE if i >= FIRST_WIDE and ob in WIDE_BLOCKS else GROUPS
-            passes = [(cp, col0, width, blocks[cp]) for cp in range(4) for col0, width, blocks in groups]
+            runs = RUNS_WIDE if i >= FIRST_WIDE else RUNS
+            passes = [(cp, col0, width, place) for cp in range(4) for col0, width, place in runs[cp]]
             for number, (cp, col0, width, block) in enumerate(passes):
                 x_cols = slice(P * cp, P * (cp + 1))
                 w_cols = slice(P * block, P * block + width)
@@ -296,8 +299,8 @@ def tile_quaternionlinear_pa_kernel(tc, x_bytes, x_scale, wr, wi, wj, wk, bias, 
         copy_out(1, 1, held_pool)
         x_scale_out(2)
         x_quantize(2)
-        w_quantize_again(0)
-        w_quantize_again(1)
+        for ob in range(O_BLOCKS):
+            w_quantize_again(ob)
         multiply(0, 2)
         multiply(1, 2)
         multiply(0, 3)

@@ -326,7 +326,7 @@ def tile_quaternionlinear_pa_kernel(tc, x_bytes, x_scale, wr, wi, wj, wk, bias, 
                 finish(i - 1, 2)
             if more:
                 x_quantize(i + 1)
-            if held:
+            for early in range(min(2, len(held))):
                 b = held.pop(0)
                 add_bias(nc.vector, b[0], b[1])
             for ob in range(O_BLOCKS):

from contextlib import ExitStack

import concourse.mybir as mybir
from concourse.masks import make_identity

F32 = mybir.dt.float32
BF16 = mybir.dt.bfloat16
U32 = mybir.dt.uint32
U8 = mybir.dt.uint8
FP8 = mybir.dt.float8_e4m3fn
FP8X4 = mybir.dt.float8_e4m3fn_x4
MULT = mybir.AluOpType.mult
ADD = mybir.AluOpType.add

P = 128
ROWS = 1024
IQ = 512
OQ = 512
Q = 4
COLS = IQ * Q
ROW_TILES = ROWS // P
O_BLOCKS = OQ // P
FLOPS = 10 * 2 * ROWS * IQ * OQ

N_BLOCKS = 8
CODE_BLOCKS = 9
FIRST_CODE = 1
SECOND = ((0, 2), (8, 6))
FIRST_WIDE = 2
FIRST_CAST_SPLIT = 768
WARM_PASSES = 6
RUNS = (
    ((0, 128, 3), (128, 128, 1), (256, 256, 4)),
    ((0, 256, 2), (256, 256, 1)),
    ((0, 128, 7), (128, 128, 7), (256, 256, 3)),
    ((0, 128, 6), (128, 256, 5), (384, 128, 3)),
)
RUNS_WIDE = (
    ((0, 256, 0), (256, 256, 4)),
    ((0, 256, 2), (256, 256, 1)),
    ((0, 256, 7), (256, 256, 3)),
    ((0, 128, 6), (128, 256, 5), (384, 128, 3)),
)


def tile_quaternionlinear_pa_kernel(tc, x_bytes, x_scale, wr, wi, wj, wk, bias, out):
    nc = tc.nc
    x_rows = x_bytes.flatten_outer_dims()
    out_rows = out.flatten_outer_dims()
    weights = (wr, wj, wi, wk)

    with ExitStack() as ctx:
        const = ctx.enter_context(tc.tile_pool(name="const", bufs=1))
        xb_pool = ctx.enter_context(tc.tile_pool(name="xb_pool", bufs=3))
        xp_pool = ctx.enter_context(tc.tile_pool(name="xp_pool", bufs=2))
        xg_pool = ctx.enter_context(tc.tile_pool(name="xg_pool", bufs=2))
        xc_pool = ctx.enter_context(tc.tile_pool(name="xc_pool", bufs=3))
        res_pool = ctx.enter_context(tc.tile_pool(name="res_pool", bufs=10))
        held_pool = ctx.enter_context(tc.tile_pool(name="held_pool", bufs=4))
        psum = ctx.enter_context(tc.psum_pool(name="psum", bufs=8))
        ctx.enter_context(tc.manual_schedule())

        ident = const.tile([P, P], F32, name="ident")
        scale16 = const.tile([P, 16], F32, name="scale16")
        zeros = const.tile([P, 512], BF16, name="zeros")
        bias_all = const.tile([P, COLS], BF16, name="bias_all")
        x_codes_in = [const.tile([P, COLS], U8, name="x_codes_in_%d" % i) for i in range(ROW_TILES)]
        w_raw = [const.tile([P, 4, IQ], BF16, name="w_raw_%d" % ob) for ob in range(O_BLOCKS)]
        w_grouped = [
            const.tile([P, N_BLOCKS * 512], BF16, name="w_grouped_%d" % ob, align_bytes=64)
            for ob in range(O_BLOCKS)
        ]
        w_codes = [
            const.tile([P, CODE_BLOCKS * P], U32, name="w_codes_%d" % ob, align_bytes=256)
            for ob in range(O_BLOCKS)
        ]
        w_scales = [
            const.tile([P, CODE_BLOCKS * P], U8, name="w_scales_%d" % ob, align_bytes=256)
            for ob in range(O_BLOCKS)
        ]

        def load_x(i):
            nc.sync.dma_start(out=x_codes_in[i][:], in_=x_rows[P * i : P * (i + 1), :])

        def load_w(ob):
            for s in range(4):
                nc.sync.dma_start(out=w_raw[ob][:, s, :], in_=weights[s][P * ob : P * (ob + 1), :])

        nc.gpsimd.memset(zeros[:], 0.0)
        make_identity(nc, ident[:])
        load_x(0)
        nc.sync.dma_start(out=scale16[:], in_=x_scale.rearrange("a b (p e) -> (a b p) e", e=16))
        load_x(1)
        load_w(0)
        load_w(1)
        load_w(2)
        load_w(3)
        load_x(2)
        load_x(3)
        nc.sync.dma_start(out=bias_all[:], in_=bias.partition_broadcast(P))
        for i in range(4, ROW_TILES):
            load_x(i)

        scale_views = [
            scale16[:].rearrange("p (t h e) -> p h e t", h=2, e=2)[:, h].unsqueeze(2).to_broadcast([P, 2, P, 4])
            for h in range(2)
        ]

        xb = {}
        xt = {}
        xp = {}
        xg = {}
        xc = {}
        xs = {}
        wt = {}
        acc = {}

        def cast(i):
            xb[i] = xb_pool.tile([P, COLS], BF16, name="xb", tag="xb")
            codes = x_codes_in[i][:].bitcast(FP8)
            split = FIRST_CAST_SPLIT if i == 0 else COLS
            nc.scalar.copy(out=xb[i][:, 0:split], in_=codes[:, 0:split])
            if split < COLS:
                nc.vector.tensor_copy(out=xb[i][:, split:COLS], in_=codes[:, split:COLS])

        def regroup(i):
            xp[i] = xp_pool.tile([P, 8, P], F32, name="xp", tag="xp")
            nc.scalar.copy(out=xp[i][:], in_=xb[i][:].bitcast(F32).rearrange("p (j q) -> p q j", q=8))

        def x_transpose(i):
            words = xb[i][:].bitcast(F32)
            xt[i] = []
            for h in range(2):
                bank = psum.tile([P, 4, P], F32, name="bank", tag="bank")
                for t in range(4):
                    if i in xp:
                        nc.tensor.transpose(bank[:, t, :], xp[i][:, 2 * t + h, :], ident[:])
                    else:
                        nc.tensor.transpose(bank[:, t, :], words[:, 2 * t + h : COLS // 2 : 8], ident[:])
                xt[i].append(bank)

        def x_scale_out(i):
            xg[i] = xg_pool.tile([P, COLS], BF16, name="xg", tag="xg", align_bytes=64)
            grouped = xg[i][:].rearrange("p (c n t) -> p c n t", c=4, t=4)
            for h in range(2):
                halves = xt[i][h][:].rearrange("p t n -> p (t n)").bitcast(BF16)
                nc.vector.tensor_tensor(
                    out=grouped[:, 2 * h : 2 * h + 2],
                    in0=halves.rearrange("p (t n e) -> p e n t", t=4, e=2),
                    in1=scale_views[h],
                    op=MULT,
                )

        def x_quantize(i):
            xc[i] = xc_pool.tile([P, 4 * P], U32, name="xc", tag="xc", align_bytes=256)
            xs[i] = xc_pool.tile([P, 4 * P], U8, name="xs", tag="xs", align_bytes=256)
            parts = 2 if i < 3 else 1
            for part in range(parts):
                cols = slice(4 * P // parts * part, 4 * P // parts * (part + 1))
                nc.vector.quantize_mx(
                    out=xc[i][:, cols].bitcast(FP8X4),
                    scales=xs[i][:, cols],
                    in_=xg[i][:, 4 * cols.start : 4 * cols.stop],
                )

        def w_transpose(ob):
            wt[ob] = []
            for b in range(2):
                bank = psum.tile([P, 4, P], F32, name="bank", tag="bank")
                for s2 in range(2):
                    words = w_raw[ob][:, 2 * b + s2, :].bitcast(F32)
                    for u in range(2):
                        nc.tensor.transpose(bank[:, 2 * s2 + u, :], words[:, u : IQ // 2 : 2], ident[:])
                wt[ob].append(bank)

        def w_out(ob):
            words = w_grouped[ob][:].bitcast(F32)
            outs = (
                words[:, 512:1024].rearrange("p (s o u) -> p s o u", s=2, u=2),
                words.rearrange("p (s x) -> p s x", s=2)[:, :, 0:256].rearrange("p s (o u) -> p s o u", u=2),
            )
            for b in range(2):
                nc.scalar.copy(out=outs[b], in_=wt[ob][b][:].rearrange("p (s u) o -> p s o u", s=2))

        def w_negate(ob):
            g = w_grouped[ob]
            halves = g[:].rearrange("p (s x) -> p s x", s=2)
            nc.vector.tensor_scalar(out=halves[:, :, 512:1024], in0=halves[:, :, 0:512], scalar1=-1.0, scalar2=None, op0=MULT)
            nc.vector.tensor_scalar(out=g[:, 3072:3584], in0=g[:, 1536:2048], scalar1=-1.0, scalar2=None, op0=MULT)

        def w_quantize(ob):
            for first, count in ((2, 4), (0, 2), (6, 1)):
                cols = slice((FIRST_CODE + first) * P, (FIRST_CODE + first + count) * P)
                nc.vector.quantize_mx(
                    out=w_codes[ob][:, cols].bitcast(FP8X4),
                    scales=w_scales[ob][:, cols],
                    in_=w_grouped[ob][:, first * 512 : (first + count) * 512],
                )

        def w_quantize_again(ob):
            for place, block in SECOND:
                cols = slice(place * P, (place + 1) * P)
                nc.vector.quantize_mx(
                    out=w_codes[ob][:, cols].bitcast(FP8X4),
                    scales=w_scales[ob][:, cols],
                    in_=w_grouped[ob][:, block * 512 : (block + 1) * 512],
                )

        def reserve(i, ob):
            acc[(i, ob)] = psum.tile([P, 512], F32, name="bank", tag="bank")

        def multiply(i, ob):
            if (i, ob) not in acc:
                reserve(i, ob)
            bank = acc[(i, ob)]
            runs = RUNS_WIDE if i >= FIRST_WIDE else RUNS
            passes = [(cp, col0, width, place) for cp in range(4) for col0, width, place in runs[cp]]
            for number, (cp, col0, width, block) in enumerate(passes):
                x_cols = slice(P * cp, P * (cp + 1))
                w_cols = slice(P * block, P * block + width)
                nc.tensor.matmul_mx(
                    out=bank[:, col0 : col0 + width],
                    lhsT=xc[i][:, x_cols].bitcast(FP8X4),
                    lhsT_scale=xs[i][:, x_cols],
                    rhs=w_codes[ob][:, w_cols].bitcast(FP8X4),
                    rhs_scale=w_scales[ob][:, w_cols],
                    start=(number == 0),
                    stop=(number == len(passes) - 1),
                )

        res = {}

        def store(i, ob):
            nc.sync.dma_start(out=out_rows[P * i : P * (i + 1), 512 * ob : 512 * (ob + 1)], in_=res[(i, ob)][:])

        def finish(i, ob):
            res[(i, ob)] = res_pool.tile([P, 512], F32, name="res", tag="res")
            nc.vector.tensor_tensor(
                out=res[(i, ob)][:].rearrange("p (o c) -> p o c", c=4),
                in0=acc[(i, ob)][:].rearrange("p (c o) -> p o c", c=4),
                in1=bias_all[:, 512 * ob : 512 * (ob + 1)].rearrange("p (o c) -> p o c", c=4),
                op=ADD,
            )
            store(i, ob)

        def copy_out(i, ob, pool):
            res[(i, ob)] = pool.tile([P, 512], F32, name="res", tag="res")
            nc.scalar.copy(
                out=res[(i, ob)][:].rearrange("p (o c) -> p o c", c=4),
                in_=acc[(i, ob)][:].rearrange("p (c o) -> p o c", c=4),
            )

        def add_bias(engine, i, ob):
            engine.tensor_tensor(
                out=res[(i, ob)][:], in0=res[(i, ob)][:], in1=bias_all[:, 512 * ob : 512 * (ob + 1)], op=ADD
            )
            store(i, ob)

        warm = psum.tile([P, 512], F32, name="bank", tag="bank")
        for w_pass in range(WARM_PASSES):
            nc.tensor.matmul(out=warm[:], lhsT=zeros[:, 0:P], rhs=zeros[:], start=True, stop=True)
        cast(0)
        x_transpose(0)
        cast(1)
        w_transpose(0)
        w_out(0)
        x_scale_out(0)
        x_quantize(0)
        w_negate(0)
        w_quantize(0)
        w_transpose(1)
        w_out(1)
        w_negate(1)
        w_quantize(1)
        x_transpose(1)
        w_transpose(2)
        w_out(2)
        cast(2)
        w_transpose(3)
        w_out(3)
        x_scale_out(1)
        x_quantize(1)
        multiply(0, 0)
        multiply(0, 1)
        reserve(1, 0)
        reserve(1, 1)
        x_transpose(2)
        w_negate(2)
        w_quantize(2)
        w_negate(3)
        w_quantize(3)
        copy_out(0, 0, held_pool)
        copy_out(0, 1, held_pool)
        cast(3)
        regroup(3)
        multiply(1, 0)
        multiply(1, 1)
        copy_out(1, 0, held_pool)
        copy_out(1, 1, held_pool)
        x_scale_out(2)
        x_quantize(2)
        for ob in range(O_BLOCKS):
            w_quantize_again(ob)
        multiply(0, 2)
        multiply(1, 2)
        multiply(0, 3)
        multiply(1, 3)
        finish(0, 2)
        finish(1, 2)
        copy_out(0, 3, res_pool)
        add_bias(nc.gpsimd, 0, 3)
        held = [(0, 0), (0, 1), (1, 0), (1, 1)]

        for i in range(2, ROW_TILES):
            more = i + 1 < ROW_TILES
            if more:
                x_transpose(i + 1)
            copy_out(i - 1, 3, res_pool)
            add_bias(nc.gpsimd, i - 1, 3)
            if i + 2 < ROW_TILES:
                cast(i + 2)
                regroup(i + 2)
            if more:
                x_scale_out(i + 1)
            if i > 2:
                finish(i - 1, 2)
            if more:
                x_quantize(i + 1)
            for early in range(min(2, len(held))):
                b = held.pop(0)
                add_bias(nc.vector, b[0], b[1])
            for ob in range(O_BLOCKS):
                multiply(i, ob)
            finish(i, 0)
            finish(i, 1)
        finish(ROW_TILES - 1, 2)
        last = (ROW_TILES - 1, O_BLOCKS - 1)
        res[last] = res_pool.tile([P, 512], F32, name="res", tag="res")
        for half in range(2):
            o_part = slice(64 * half, 64 * (half + 1))
            cols = slice(256 * half, 256 * (half + 1))
            first = 512 * last[1] + 256 * half
            nc.vector.tensor_tensor(
                out=res[last][:, cols].rearrange("p (o c) -> p o c", c=4),
                in0=acc[last][:].rearrange("p (c o) -> p o c", c=4)[:, o_part, :],
                in1=bias_all[:, first : first + 256].rearrange("p (o c) -> p o c", c=4),
                op=ADD,
            )
            nc.sync.dma_start(out=out_rows[P * last[0] : P * (last[0] + 1), first : first + 256], in_=res[last][:, cols])
